import numpy as np
import ml_dtypes


def mxq(x, axis, fmt="e4m3"):
    dtype, down = {"e4m3": (ml_dtypes.float8_e4m3fn, 7), "e5m2": (ml_dtypes.float8_e5m2, 14)}[fmt]
    v = np.moveaxis(np.asarray(x, np.float32).astype(ml_dtypes.bfloat16).astype(np.float64), axis, -1)
    blocks = v.reshape(v.shape[:-1] + (-1, 32))
    amax = np.abs(blocks).max(-1, keepdims=True)
    byte = np.maximum(np.where(amax > 0, np.frexp(amax)[1] - 1 + 127, 0) - down, 1)
    scale = np.exp2(byte - 127.0)
    codes = (blocks / scale).astype(np.float32).astype(dtype).astype(np.float64)
    return np.moveaxis((codes * scale).reshape(v.shape), -1, axis)


WIDE = False


def mx_kscale(k):
    if not WIDE:
        return np.ones(k)
    levels = np.array([10, -10, 5, -5, 0])
    a = np.random.permutation(np.resize(levels, k // 512 * 4)).reshape(k // 512, 4)
    idx = np.arange(k)
    return np.exp2(a[idx // 512, idx % 128 // 32])


BF16 = ml_dtypes.bfloat16


def bf(x):
    return np.asarray(x, np.float32).astype(BF16)


def f64(x):
    return np.asarray(x).astype(np.float64)


B, T, C, H, D, R = 4, 1024, 1024, 8, 128, 512
EPS = 1e-6
THETA = 10000.0


def rmsnorm(v, w):
    var = np.mean(v * v, axis=-1, keepdims=True)
    return v * (1.0 / np.sqrt(var + EPS)) * w


def rope(v, cos, sin):
    re, im = v[..., 0::2], v[..., 1::2]
    c, s = cos[None, :, None, :], sin[None, :, None, :]
    return np.stack([re * c - im * s, re * s + im * c], axis=-1).reshape(v.shape)


def setup_inputs():
    s = mx_kscale(C)
    ang = np.outer(np.arange(T), 1.0 / THETA ** (np.arange(0, D, 2) / D))
    return {"x": bf(np.random.standard_normal((B, T, C)) * s),
            "wq": bf(np.random.standard_normal((H * D, C)) / np.sqrt(C) / s[None, :]),
            "q_norm_w": bf(1.0 + 0.1 * np.random.standard_normal(D)),
            "freqs_cos": bf(np.cos(ang)), "freqs_sin": bf(np.sin(ang))}


def reference(x, wq, q_norm_w, freqs_cos, freqs_sin):
    xq = (mxq(f64(x), 2, "e4m3") @ mxq(f64(wq), 1, "e4m3").T).reshape(B, T, H, D)
    return rope(rmsnorm(xq, f64(q_norm_w)), f64(freqs_cos), f64(freqs_sin))

@@ -1,0 +1,227 @@
+from contextlib import ExitStack
+
+import concourse.mybir as mybir
+from concourse.masks import make_identity
+
+F32 = mybir.dt.float32
+BF16 = mybir.dt.bfloat16
+U32 = mybir.dt.uint32
+U8 = mybir.dt.uint8
+FP8X4 = mybir.dt.float8_e4m3fn_x4
+ACT = mybir.ActivationFunctionType
+ALU = mybir.AluOpType
+
+P = 128
+TOKENS = 4 * 1024
+SEQUENCE = 1024
+K = 1024
+HEADS = 8
+HEAD_DIM = 128
+PAIRS = HEAD_DIM // 2
+FEATURES = HEADS * HEAD_DIM
+EPS = 1e-6
+
+PACK = 4
+PASSES = K // (P * PACK)
+HALVES = 2
+WORD_BLOCKS = PASSES * HALVES
+BANK = 512
+BANKS = FEATURES // BANK
+HEADS_PER_BANK = BANK // HEAD_DIM
+GROUP = 4
+TILES = TOKENS // P
+TABLES = SEQUENCE // P
+
+FLOPS = 2 * TOKENS * K * FEATURES
+
+
+def tile_mla_pb_t_kernel(tc, x, wq, q_norm_w, freqs_cos, freqs_sin, out):
+    nc = tc.nc
+    x_rows = x.flatten_outer_dims()
+    out_rows = out.rearrange("b t h d -> (b t) (h d)")
+
+    with ExitStack() as stack:
+        keep = stack.enter_context(tc.tile_pool(name="keep", bufs=1))
+        stage = stack.enter_context(tc.tile_pool(name="stage", bufs=2))
+        work = stack.enter_context(tc.tile_pool(name="work", bufs=3))
+        psum_turned = stack.enter_context(tc.psum_pool(name="psum_turned", bufs=2))
+        psum_q = stack.enter_context(tc.psum_pool(name="psum_q", bufs=3 * BANKS))
+        stack.enter_context(tc.manual_schedule())
+
+        gain = keep.tile([P, HEAD_DIM], BF16)
+        nc.scalar.dma_start(out=gain[:], in_=q_norm_w.partition_broadcast(P))
+        cos = keep.tile([P, TABLES // GROUP, GROUP * PAIRS], BF16)
+        sin = keep.tile([P, TABLES // GROUP, GROUP * PAIRS], BF16)
+        for table, freqs in ((cos, freqs_cos), (sin, freqs_sin)):
+            nc.scalar.dma_start(out=table[:], in_=freqs.rearrange("(s p i) j -> p s (i j)", p=P, i=GROUP))
+
+        wq_sb = keep.tile([P, HEADS, K], BF16)
+        wq_by_head = wq.rearrange("(h p) k -> p h k", p=P)
+        for h in range(0, HEADS, 2):
+            nc.sync.dma_start(out=wq_sb[:, h : h + 2, :], in_=wq_by_head[:, h : h + 2, :])
+        x_sb = keep.tile([P, TILES, K], BF16)
+        for first in range(0, TILES, GROUP):
+            nc.sync.dma_start(
+                out=x_sb[:, first : first + GROUP, :],
+                in_=x_rows[first * P : (first + GROUP) * P, :].rearrange("(p i) k -> p i k", i=GROUP),
+            )
+
+        eps = keep.tile([P, 1], F32)
+        nc.vector.memset(eps[:], EPS)
+        first_sqrt = keep.tile([P, 1], F32)
+        nc.scalar.activation(out=first_sqrt[:], in_=eps[:], func=ACT.Sqrt)
+
+        identity = keep.tile([P, P], F32)
+        make_identity(nc, identity[:])
+        evens_first = keep.tile([P, P], F32)
+        nc.vector.tensor_copy(
+            out=evens_first[:].rearrange("p (a j) -> p a j", a=2),
+            in_=identity[:].rearrange("p (j a) -> p a j", a=2),
+        )
+
+        neg_sin = keep.tile([P, TABLES // GROUP, GROUP * PAIRS], BF16)
+        nc.gpsimd.tensor_scalar(out=neg_sin[:], in0=sin[:], scalar1=-1.0, scalar2=0.0, op0=ALU.mult, op1=ALU.add)
+        rot = keep.tile([P, TABLES, 2 * HEAD_DIM], F32)
+        rot_parts = rot[:].rearrange("p m (e a j) -> p e a m j", e=2, a=2)
+        gain_parts = gain[:].rearrange("p (j a) -> p a j", a=2)
+        for e, a, trig in ((0, 0, cos), (0, 1, neg_sin), (1, 0, sin), (1, 1, cos)):
+            nc.gpsimd.tensor_tensor(
+                out=rot_parts[:, e, a],
+                in0=trig[:].rearrange("p s (i j) -> p (s i) j", i=GROUP),
+                in1=gain_parts[:, a].unsqueeze(1).to_broadcast([P, TABLES, PAIRS]),
+                op=ALU.mult,
+            )
+
+        def turn(rows, selector):
+            turned = psum_turned.tile([P, WORD_BLOCKS, P], F32)
+            words = rows.bitcast(F32)
+            for w in range(WORD_BLOCKS):
+                nc.tensor.transpose(turned[:, w, :], words[:, w * P : (w + 1) * P], selector[:])
+            return turned
+
+        def by_packed_word(turned):
+            return turned[:].rearrange("p (g u) r -> p g r u", u=HALVES)
+
+        w_grouped = keep.tile([P, PASSES, FEATURES, PACK], BF16, align_bytes=64)
+        w_words = w_grouped[:].rearrange("p g f t -> p (g f t)").bitcast(F32)
+        w_words = w_words.rearrange("p (g f u) -> p g f u", g=PASSES, u=HALVES)
+        w_codes = keep.tile([P, PASSES, FEATURES], U32, align_bytes=64)
+        w_scales = keep.tile([P, PASSES, FEATURES], U8, align_bytes=64)
+        for h in range(HEADS):
+            turned = turn(wq_sb[:, h, :], evens_first)
+            columns = w_words[:, :, h * HEAD_DIM : (h + 1) * HEAD_DIM, :]
+            if h % 2 == 0:
+                nc.scalar.copy(out=columns, in_=by_packed_word(turned))
+            else:
+                nc.vector.tensor_copy(out=columns, in_=by_packed_word(turned))
+            if h % HEADS_PER_BANK == HEADS_PER_BANK - 1:
+                features = slice((h + 1) * HEAD_DIM - BANK, (h + 1) * HEAD_DIM)
+                for g in range(PASSES):
+                    nc.vector.quantize_mx(
+                        out=w_codes[:, g, features].bitcast(FP8X4),
+                        scales=w_scales[:, g, features],
+                        in_=w_grouped[:, g, features, :].rearrange("p f t -> p (f t)"),
+                    )
+
+        turned_of, grouped_of, codes_of, scales_of = {}, {}, {}, {}
+        q_of, squares_of, rms_of, inverse_of = {}, {}, {}, {}
+
+        def transpose_x(n):
+            turned_of[n] = turn(x_sb[:, n, :], identity)
+
+        def regroup_x(n):
+            x_grouped = stage.tile([P, PASSES * P * PACK], BF16, align_bytes=64)
+            nc.scalar.copy(
+                out=x_grouped[:].bitcast(F32).rearrange("p (g r u) -> p g r u", g=PASSES, u=HALVES),
+                in_=by_packed_word(turned_of[n]),
+            )
+            grouped_of[n] = x_grouped
+
+        def quantise_x(n):
+            x_codes = stage.tile([P, PASSES * P], U32, align_bytes=64)
+            x_scales = stage.tile([P, PASSES * P], U8, align_bytes=64)
+            nc.vector.quantize_mx(out=x_codes[:].bitcast(FP8X4), scales=x_scales[:], in_=grouped_of[n][:])
+            codes_of[n], scales_of[n] = x_codes, x_scales
+
+        def multiply(n):
+            x_codes, x_scales = codes_of[n], scales_of[n]
+            q_of[n] = []
+            for b in range(BANKS):
+                q_bank = psum_q.tile([P, BANK], F32)
+                features = slice(b * BANK, (b + 1) * BANK)
+                for g in range(PASSES):
+                    tokens = slice(g * P, (g + 1) * P)
+                    nc.tensor.matmul_mx(
+                        out=q_bank[:],
+                        lhsT=x_codes[:, tokens].bitcast(FP8X4),
+                        lhsT_scale=x_scales[:, tokens],
+                        rhs=w_codes[:, g, features].bitcast(FP8X4),
+                        rhs_scale=w_scales[:, g, features],
+                        start=(g == 0),
+                        stop=(g == PASSES - 1),
+                    )
+                q_of[n].append(q_bank)
+
+        def head(n, h):
+            column = (h % HEADS_PER_BANK) * HEAD_DIM
+            return q_of[n][h // HEADS_PER_BANK][:, column : column + HEAD_DIM]
+
+        def sum_squares(n):
+            squares = stage.tile([P, HEADS], F32)
+            unread = stage.tile([P, FEATURES], BF16)
+            for h in range(HEADS):
+                nc.scalar.activation(
+                    out=unread[:, h * HEAD_DIM : (h + 1) * HEAD_DIM],
+                    in_=head(n, h),
+                    func=ACT.Square,
+                    accum_out=squares[:, h : h + 1],
+                )
+            squares_of[n] = squares
+
+        def root(n):
+            rms = stage.tile([P, HEADS], F32)
+            nc.scalar.activation(out=rms[:], in_=squares_of[n][:], func=ACT.Sqrt, scale=1.0 / HEAD_DIM, bias=eps[:])
+            rms_of[n] = rms
+
+        def invert(n):
+            inverse = stage.tile([P, HEADS], F32)
+            nc.vector.reciprocal(out=inverse[:], in_=rms_of[n][:])
+            inverse_of[n] = inverse
+
+        def rotate(n):
+            inverse = inverse_of[n]
+            products = work.tile([P, HEADS, 2 * HEAD_DIM], F32)
+            for h in range(HEADS):
+                nc.vector.scalar_tensor_tensor(
+                    out=products[:, h, :].rearrange("p (e c) -> p e c", e=2),
+                    in0=head(n, h).unsqueeze(1).to_broadcast([P, 2, HEAD_DIM]),
+                    scalar=inverse[:, h : h + 1],
+                    in1=rot[:, n % TABLES, :].rearrange("p (e c) -> p e c", e=2),
+                    op0=ALU.mult,
+                    op1=ALU.mult,
+                )
+            rotated = work.tile([P, FEATURES], F32)
+            parts = products[:].rearrange("p h (e a j) -> p a h j e", e=2, a=2)
+            nc.gpsimd.tensor_tensor(
+                out=rotated[:].rearrange("p (h j e) -> p h j e", h=HEADS, e=2),
+                in0=parts[:, 0],
+                in1=parts[:, 1],
+                op=ALU.add,
+            )
+            first = n - n % GROUP
+            group_rows = out_rows[first * P : (first + GROUP) * P, :].rearrange("(p i) f -> p i f", i=GROUP)
+            nc.sync.dma_start(out=group_rows[:, n % GROUP, :], in_=rotated[:])
+
+        def when_valid(stage_of_tile, n):
+            if 0 <= n < TILES:
+                stage_of_tile(n)
+
+        for step in range(-4, TILES):
+            when_valid(transpose_x, step + 4)
+            when_valid(invert, step)
+            when_valid(quantise_x, step + 2)
+            when_valid(multiply, step + 2)
+            when_valid(sum_squares, step + 1)
+            when_valid(regroup_x, step + 3)
+            when_valid(root, step + 1)
+            when_valid(rotate, step)

@@ -82,7 +82,7 @@ def tile_mla_pb_t_kernel(tc, x, wq, q_norm_w, freqs_cos, freqs_sin, out):
         neg_sin = keep.tile([P, TABLES // GROUP, GROUP * PAIRS], BF16)
         nc.gpsimd.tensor_scalar(out=neg_sin[:], in0=sin[:], scalar1=-1.0, scalar2=0.0, op0=ALU.mult, op1=ALU.add)
         rot = keep.tile([P, TABLES, 2 * HEAD_DIM], F32)
-        rot_parts = rot[:].rearrange("p m (e a j) -> p e a m j", e=2, a=2)
+        rot_parts = rot[:].rearrange("p m (a j e) -> p e a m j", a=2, e=2)
         gain_parts = gain[:].rearrange("p (j a) -> p a j", a=2)
         for e, a, trig in ((0, 0, cos), (0, 1, neg_sin), (1, 0, sin), (1, 1, cos)):
             nc.gpsimd.tensor_tensor(
@@ -190,24 +190,18 @@ def tile_mla_pb_t_kernel(tc, x, wq, q_norm_w, freqs_cos, freqs_sin, out):
 
         def rotate(n):
             inverse = inverse_of[n]
-            products = work.tile([P, HEADS, 2 * HEAD_DIM], F32)
+            products = work.tile([P, 2, FEATURES], F32)
             for h in range(HEADS):
                 nc.vector.scalar_tensor_tensor(
-                    out=products[:, h, :].rearrange("p (e c) -> p e c", e=2),
-                    in0=head(n, h).unsqueeze(1).to_broadcast([P, 2, HEAD_DIM]),
+                    out=products[:, :, h * HEAD_DIM : (h + 1) * HEAD_DIM].rearrange("p a (j e) -> p a j e", e=2),
+                    in0=head(n, h).rearrange("p (a j) -> p a j", a=2).unsqueeze(3).to_broadcast([P, 2, PAIRS, 2]),
                     scalar=inverse[:, h : h + 1],
-                    in1=rot[:, n % TABLES, :].rearrange("p (e c) -> p e c", e=2),
+                    in1=rot[:, n % TABLES, :].rearrange("p (a j e) -> p a j e", a=2, e=2),
                     op0=ALU.mult,
                     op1=ALU.mult,
                 )
             rotated = work.tile([P, FEATURES], F32)
-            parts = products[:].rearrange("p h (e a j) -> p a h j e", e=2, a=2)
-            nc.gpsimd.tensor_tensor(
-                out=rotated[:].rearrange("p (h j e) -> p h j e", h=HEADS, e=2),
-                in0=parts[:, 0],
-                in1=parts[:, 1],
-                op=ALU.add,
-            )
+            nc.gpsimd.tensor_tensor(out=rotated[:], in0=products[:, 0, :], in1=products[:, 1, :], op=ALU.add)
             first = n - n % GROUP
             group_rows = out_rows[first * P : (first + GROUP) * P, :].rearrange("(p i) f -> p i f", i=GROUP)
             nc.sync.dma_start(out=group_rows[:, n % GROUP, :], in_=rotated[:])

@@ -68,8 +68,8 @@ def tile_mla_pb_t_kernel(tc, x, wq, q_norm_w, freqs_cos, freqs_sin, out):
 
         eps = keep.tile([P, 1], F32)
         nc.vector.memset(eps[:], EPS)
-        first_sqrt = keep.tile([P, 1], F32)
-        nc.scalar.activation(out=first_sqrt[:], in_=eps[:], func=ACT.Sqrt)
+        first_use = keep.tile([P, 1], F32)
+        nc.scalar.activation(out=first_use[:], in_=eps[:], func=ACT.Abs_reciprocal_sqrt)
 
         identity = keep.tile([P, P], F32)
         make_identity(nc, identity[:])
@@ -124,7 +124,7 @@ def tile_mla_pb_t_kernel(tc, x, wq, q_norm_w, freqs_cos, freqs_sin, out):
                     )
 
         turned_of, grouped_of, codes_of, scales_of = {}, {}, {}, {}
-        q_of, squares_of, rms_of, inverse_of = {}, {}, {}, {}
+        q_of, squares_of, inverse_of = {}, {}, {}
 
         def transpose_x(n):
             turned_of[n] = turn(x_sb[:, n, :], identity)
@@ -178,14 +178,11 @@ def tile_mla_pb_t_kernel(tc, x, wq, q_norm_w, freqs_cos, freqs_sin, out):
                 )
             squares_of[n] = squares
 
-        def root(n):
-            rms = stage.tile([P, HEADS], F32)
-            nc.scalar.activation(out=rms[:], in_=squares_of[n][:], func=ACT.Sqrt, scale=1.0 / HEAD_DIM, bias=eps[:])
-            rms_of[n] = rms
-
-        def invert(n):
+        def inverse_rms(n):
             inverse = stage.tile([P, HEADS], F32)
-            nc.vector.reciprocal(out=inverse[:], in_=rms_of[n][:])
+            nc.scalar.activation(
+                out=inverse[:], in_=squares_of[n][:], func=ACT.Abs_reciprocal_sqrt, scale=1.0 / HEAD_DIM, bias=eps[:]
+            )
             inverse_of[n] = inverse
 
         def rotate(n):
@@ -212,10 +209,9 @@ def tile_mla_pb_t_kernel(tc, x, wq, q_norm_w, freqs_cos, freqs_sin, out):
 
         for step in range(-4, TILES):
             when_valid(transpose_x, step + 4)
-            when_valid(invert, step)
             when_valid(quantise_x, step + 2)
             when_valid(multiply, step + 2)
             when_valid(sum_squares, step + 1)
             when_valid(regroup_x, step + 3)
-            when_valid(root, step + 1)
+            when_valid(inverse_rms, step + 1)
             when_valid(rotate, step)

@@ -44,12 +44,14 @@ def tile_mla_pb_t_kernel(tc, x, wq, q_norm_w, freqs_cos, freqs_sin, out):
         keep = stack.enter_context(tc.tile_pool(name="keep", bufs=1))
         stage = stack.enter_context(tc.tile_pool(name="stage", bufs=2))
         work = stack.enter_context(tc.tile_pool(name="work", bufs=3))
+        results = stack.enter_context(tc.tile_pool(name="results", bufs=4))
         psum_turned = stack.enter_context(tc.psum_pool(name="psum_turned", bufs=2))
         psum_q = stack.enter_context(tc.psum_pool(name="psum_q", bufs=3 * BANKS))
         stack.enter_context(tc.manual_schedule())
 
-        gain = keep.tile([P, HEAD_DIM], BF16)
-        nc.scalar.dma_start(out=gain[:], in_=q_norm_w.partition_broadcast(P))
+        gain_row = keep.tile([P, HEAD_DIM], BF16)
+        nc.vector.memset(gain_row[:], 0.0)
+        nc.sync.dma_start(out=gain_row[0:1, :], in_=q_norm_w.unsqueeze(0))
         cos = keep.tile([P, TABLES // GROUP, GROUP * PAIRS], BF16)
         sin = keep.tile([P, TABLES // GROUP, GROUP * PAIRS], BF16)
         for table, freqs in ((cos, freqs_cos), (sin, freqs_sin)):
@@ -57,14 +59,16 @@ def tile_mla_pb_t_kernel(tc, x, wq, q_norm_w, freqs_cos, freqs_sin, out):
 
         wq_sb = keep.tile([P, HEADS, K], BF16)
         wq_by_head = wq.rearrange("(h p) k -> p h k", p=P)
-        for h in range(0, HEADS, 2):
-            nc.sync.dma_start(out=wq_sb[:, h : h + 2, :], in_=wq_by_head[:, h : h + 2, :])
+        for h in range(HEADS):
+            nc.sync.dma_start(out=wq_sb[:, h, :], in_=wq_by_head[:, h, :])
         x_sb = keep.tile([P, TILES, K], BF16)
         for first in range(0, TILES, GROUP):
-            nc.sync.dma_start(
-                out=x_sb[:, first : first + GROUP, :],
-                in_=x_rows[first * P : (first + GROUP) * P, :].rearrange("(p i) k -> p i k", i=GROUP),
-            )
+            x_group = x_rows[first * P : (first + GROUP) * P, :].rearrange("(p i) k -> p i k", i=GROUP)
+            if first == 0:
+                for i in range(GROUP):
+                    nc.sync.dma_start(out=x_sb[:, i, :], in_=x_group[:, i, :])
+            else:
+                nc.sync.dma_start(out=x_sb[:, first : first + GROUP, :], in_=x_group)
 
         eps = keep.tile([P, 1], F32)
         nc.vector.memset(eps[:], EPS)
@@ -78,6 +82,13 @@ def tile_mla_pb_t_kernel(tc, x, wq, q_norm_w, freqs_cos, freqs_sin, out):
             out=evens_first[:].rearrange("p (a j) -> p a j", a=2),
             in_=identity[:].rearrange("p (j a) -> p a j", a=2),
         )
+
+        ones = keep.tile([P, P], BF16)
+        nc.vector.memset(ones[:], 1.0)
+        gain_bank = psum_turned.tile([P, WORD_BLOCKS, P], F32, tag="turned")
+        nc.tensor.matmul(out=gain_bank[:, 0, :], lhsT=ones[:], rhs=gain_row[:], start=True, stop=True)
+        gain = keep.tile([P, HEAD_DIM], F32)
+        nc.vector.tensor_copy(out=gain[:], in_=gain_bank[:, 0, :])
 
         neg_sin = keep.tile([P, TABLES // GROUP, GROUP * PAIRS], BF16)
         nc.gpsimd.tensor_scalar(out=neg_sin[:], in0=sin[:], scalar1=-1.0, scalar2=0.0, op0=ALU.mult, op1=ALU.add)
@@ -102,26 +113,35 @@ def tile_mla_pb_t_kernel(tc, x, wq, q_norm_w, freqs_cos, freqs_sin, out):
         def by_packed_word(turned):
             return turned[:].rearrange("p (g u) r -> p g r u", u=HALVES)
 
-        w_grouped = keep.tile([P, PASSES, FEATURES, PACK], BF16, align_bytes=64)
-        w_words = w_grouped[:].rearrange("p g f t -> p (g f t)").bitcast(F32)
-        w_words = w_words.rearrange("p (g f u) -> p g f u", g=PASSES, u=HALVES)
         w_codes = keep.tile([P, PASSES, FEATURES], U32, align_bytes=64)
         w_scales = keep.tile([P, PASSES, FEATURES], U8, align_bytes=64)
-        for h in range(HEADS):
+
+        w_grouped_of = {}
+
+        def regroup_w(h):
             turned = turn(wq_sb[:, h, :], evens_first)
-            columns = w_words[:, :, h * HEAD_DIM : (h + 1) * HEAD_DIM, :]
+            w_grouped = work.tile([P, PASSES * HEAD_DIM * PACK], BF16, align_bytes=64)
+            words = w_grouped[:].bitcast(F32).rearrange("p (g r u) -> p g r u", g=PASSES, u=HALVES)
             if h % 2 == 0:
-                nc.scalar.copy(out=columns, in_=by_packed_word(turned))
+                nc.scalar.copy(out=words, in_=by_packed_word(turned))
             else:
-                nc.vector.tensor_copy(out=columns, in_=by_packed_word(turned))
-            if h % HEADS_PER_BANK == HEADS_PER_BANK - 1:
-                features = slice((h + 1) * HEAD_DIM - BANK, (h + 1) * HEAD_DIM)
-                for g in range(PASSES):
-                    nc.vector.quantize_mx(
-                        out=w_codes[:, g, features].bitcast(FP8X4),
-                        scales=w_scales[:, g, features],
-                        in_=w_grouped[:, g, features, :].rearrange("p f t -> p (f t)"),
-                    )
+                nc.vector.tensor_copy(out=words, in_=by_packed_word(turned))
+            w_grouped_of[h] = w_grouped
+
+        def quantise_w(h):
+            features = slice(h * HEAD_DIM, (h + 1) * HEAD_DIM)
+            for g in range(PASSES):
+                nc.vector.quantize_mx(
+                    out=w_codes[:, g, features].bitcast(FP8X4),
+                    scales=w_scales[:, g, features],
+                    in_=w_grouped_of[h][:, g * HEAD_DIM * PACK : (g + 1) * HEAD_DIM * PACK],
+                )
+
+        for h in range(HEADS + 1):
+            if h < HEADS:
+                regroup_w(h)
+            if h > 0:
+                quantise_w(h - 1)
 
         turned_of, grouped_of, codes_of, scales_of = {}, {}, {}, {}
         q_of, squares_of, inverse_of = {}, {}, {}
@@ -166,6 +186,10 @@ def tile_mla_pb_t_kernel(tc, x, wq, q_norm_w, freqs_cos, freqs_sin, out):
             column = (h % HEADS_PER_BANK) * HEAD_DIM
             return q_of[n][h // HEADS_PER_BANK][:, column : column + HEAD_DIM]
 
+        def bank_columns(products, h):
+            column = (h % HEADS_PER_BANK) * HEAD_DIM
+            return products[:, h // HEADS_PER_BANK, :, column : column + HEAD_DIM]
+
         def sum_squares(n):
             squares = stage.tile([P, HEADS], F32)
             unread = stage.tile([P, FEATURES], BF16)
@@ -178,40 +202,62 @@ def tile_mla_pb_t_kernel(tc, x, wq, q_norm_w, freqs_cos, freqs_sin, out):
                 )
             squares_of[n] = squares
 
-        def inverse_rms(n):
-            inverse = stage.tile([P, HEADS], F32)
+        def inverse_rms(n, b):
+            if b == 0:
+                inverse = stage.tile([P, HEADS], F32)
+                inverse_of[n] = inverse
+            heads = slice(b * HEADS_PER_BANK, (b + 1) * HEADS_PER_BANK)
             nc.scalar.activation(
-                out=inverse[:], in_=squares_of[n][:], func=ACT.Abs_reciprocal_sqrt, scale=1.0 / HEAD_DIM, bias=eps[:]
+                out=inverse_of[n][:, heads],
+                in_=squares_of[n][:, heads],
+                func=ACT.Abs_reciprocal_sqrt,
+                scale=1.0 / HEAD_DIM,
+                bias=eps[:],
             )
-            inverse_of[n] = inverse
+
+        def inverse_rms_first_bank(n):
+            inverse_rms(n, 0)
+
+        def inverse_rms_second_bank(n):
+            inverse_rms(n, 1)
 
         def rotate(n):
             inverse = inverse_of[n]
-            products = work.tile([P, 2, FEATURES], F32)
+            products = work.tile([P, BANKS, 2, BANK], F32)
+
+            def add_and_store(adder, first_bank, banks):
+                some = slice(first_bank, first_bank + banks)
+                rotated = results.tile([P, banks, BANK], F32)
+                adder.tensor_tensor(out=rotated[:], in0=products[:, some, 0, :], in1=products[:, some, 1, :], op=ALU.add)
+                first = n - n % GROUP
+                out_group = out_rows[first * P : (first + GROUP) * P, :].rearrange("(p i) (b f) -> p i b f", i=GROUP, f=BANK)
+                nc.sync.dma_start(out=out_group[:, n % GROUP, some, :], in_=rotated[:])
+
             for h in range(HEADS):
                 nc.vector.scalar_tensor_tensor(
-                    out=products[:, :, h * HEAD_DIM : (h + 1) * HEAD_DIM].rearrange("p a (j e) -> p a j e", e=2),
+                    out=bank_columns(products, h).rearrange("p a (j e) -> p a j e", e=2),
                     in0=head(n, h).rearrange("p (a j) -> p a j", a=2).unsqueeze(3).to_broadcast([P, 2, PAIRS, 2]),
                     scalar=inverse[:, h : h + 1],
                     in1=rot[:, n % TABLES, :].rearrange("p (a j e) -> p a j e", a=2, e=2),
                     op0=ALU.mult,
                     op1=ALU.mult,
                 )
-            rotated = work.tile([P, FEATURES], F32)
-            nc.gpsimd.tensor_tensor(out=rotated[:], in0=products[:, 0, :], in1=products[:, 1, :], op=ALU.add)
-            first = n - n % GROUP
-            group_rows = out_rows[first * P : (first + GROUP) * P, :].rearrange("(p i) f -> p i f", i=GROUP)
-            nc.sync.dma_start(out=group_rows[:, n % GROUP, :], in_=rotated[:])
+            if n < TILES - 1:
+                add_and_store(nc.gpsimd, 0, BANKS)
+            else:
+                for b in range(BANKS):
+                    add_and_store(nc.vector, b, 1)
 
         def when_valid(stage_of_tile, n):
             if 0 <= n < TILES:
                 stage_of_tile(n)
 
         for step in range(-4, TILES):
-            when_valid(transpose_x, step + 4)
             when_valid(quantise_x, step + 2)
             when_valid(multiply, step + 2)
+            when_valid(transpose_x, step + 4)
             when_valid(sum_squares, step + 1)
+            when_valid(inverse_rms_first_bank, step + 1)
             when_valid(regroup_x, step + 3)
-            when_valid(inverse_rms, step + 1)
+            when_valid(inverse_rms_second_bank, step + 1)
             when_valid(rotate, step)

@@ -29,6 +29,7 @@ BANK = 512
 BANKS = FEATURES // BANK
 HEADS_PER_BANK = BANK // HEAD_DIM
 GROUP = 4
+PAIR = 2
 TILES = TOKENS // P
 TABLES = SEQUENCE // P
 
@@ -44,7 +45,7 @@ def tile_mla_pb_t_kernel(tc, x, wq, q_norm_w, freqs_cos, freqs_sin, out):
         keep = stack.enter_context(tc.tile_pool(name="keep", bufs=1))
         stage = stack.enter_context(tc.tile_pool(name="stage", bufs=2))
         work = stack.enter_context(tc.tile_pool(name="work", bufs=3))
-        results = stack.enter_context(tc.tile_pool(name="results", bufs=4))
+        results = stack.enter_context(tc.tile_pool(name="results", bufs=6))
         psum_turned = stack.enter_context(tc.psum_pool(name="psum_turned", bufs=2))
         psum_q = stack.enter_context(tc.psum_pool(name="psum_q", bufs=3 * BANKS))
         stack.enter_context(tc.manual_schedule())
@@ -143,28 +144,35 @@ def tile_mla_pb_t_kernel(tc, x, wq, q_norm_w, freqs_cos, freqs_sin, out):
             if h > 0:
                 quantise_w(h - 1)
 
-        turned_of, grouped_of, codes_of, scales_of = {}, {}, {}, {}
-        q_of, squares_of, inverse_of = {}, {}, {}
+        turned_of, q_of, squares_of, inverse_of = {}, {}, {}, {}
+        grouped_of, codes_of, scales_of, products_of = {}, {}, {}, {}
 
         def transpose_x(n):
             turned_of[n] = turn(x_sb[:, n, :], identity)
 
         def regroup_x(n):
-            x_grouped = stage.tile([P, PASSES * P * PACK], BF16, align_bytes=64)
+            if n % PAIR == 0:
+                x_grouped = stage.tile([P, PAIR, PASSES * P * PACK], BF16, align_bytes=64)
+                grouped_of[n // PAIR] = x_grouped
             nc.scalar.copy(
-                out=x_grouped[:].bitcast(F32).rearrange("p (g r u) -> p g r u", g=PASSES, u=HALVES),
+                out=grouped_of[n // PAIR][:, n % PAIR, :].bitcast(F32).rearrange("p (g r u) -> p g r u", g=PASSES, u=HALVES),
                 in_=by_packed_word(turned_of[n]),
             )
-            grouped_of[n] = x_grouped
 
-        def quantise_x(n):
-            x_codes = stage.tile([P, PASSES * P], U32, align_bytes=64)
-            x_scales = stage.tile([P, PASSES * P], U8, align_bytes=64)
-            nc.vector.quantize_mx(out=x_codes[:].bitcast(FP8X4), scales=x_scales[:], in_=grouped_of[n][:])
-            codes_of[n], scales_of[n] = x_codes, x_scales
+        def quantise_x(n, count):
+            if n % PAIR == 0:
+                x_codes = stage.tile([P, PAIR, PASSES * P], U32, align_bytes=64)
+                x_scales = stage.tile([P, PAIR, PASSES * P], U8, align_bytes=64)
+                codes_of[n // PAIR], scales_of[n // PAIR] = x_codes, x_scales
+            tiles = slice(n % PAIR, n % PAIR + count)
+            nc.vector.quantize_mx(
+                out=codes_of[n // PAIR][:, tiles, :].rearrange("p i c -> p (i c)").bitcast(FP8X4),
+                scales=scales_of[n // PAIR][:, tiles, :].rearrange("p i c -> p (i c)"),
+                in_=grouped_of[n // PAIR][:, tiles, :].rearrange("p i c -> p (i c)"),
+            )
 
         def multiply(n):
-            x_codes, x_scales = codes_of[n], scales_of[n]
+            x_codes, x_scales = codes_of[n // PAIR][:, n % PAIR, :], scales_of[n // PAIR][:, n % PAIR, :]
             q_of[n] = []
             for b in range(BANKS):
                 q_bank = psum_q.tile([P, BANK], F32)
@@ -186,9 +194,6 @@ def tile_mla_pb_t_kernel(tc, x, wq, q_norm_w, freqs_cos, freqs_sin, out):
             column = (h % HEADS_PER_BANK) * HEAD_DIM
             return q_of[n][h // HEADS_PER_BANK][:, column : column + HEAD_DIM]
 
-        def bank_columns(products, h):
-            column = (h % HEADS_PER_BANK) * HEAD_DIM
-            return products[:, h // HEADS_PER_BANK, :, column : column + HEAD_DIM]
 
         def sum_squares(n):
             squares = stage.tile([P, HEADS], F32)
@@ -223,41 +228,54 @@ def tile_mla_pb_t_kernel(tc, x, wq, q_norm_w, freqs_cos, freqs_sin, out):
 
         def rotate(n):
             inverse = inverse_of[n]
-            products = work.tile([P, BANKS, 2, BANK], F32)
+            if n % PAIR == 0:
+                new_products = work.tile([P, PAIR * BANKS, 2, BANK], F32)
+                products_of[n // PAIR] = new_products
+            products = products_of[n // PAIR]
 
             def add_and_store(adder, first_bank, banks):
-                some = slice(first_bank, first_bank + banks)
+                chosen = slice(first_bank, first_bank + banks)
                 rotated = results.tile([P, banks, BANK], F32)
-                adder.tensor_tensor(out=rotated[:], in0=products[:, some, 0, :], in1=products[:, some, 1, :], op=ALU.add)
+                adder.tensor_tensor(out=rotated[:], in0=products[:, chosen, 0, :], in1=products[:, chosen, 1, :], op=ALU.add)
                 first = n - n % GROUP
-                out_group = out_rows[first * P : (first + GROUP) * P, :].rearrange("(p i) (b f) -> p i b f", i=GROUP, f=BANK)
-                nc.sync.dma_start(out=out_group[:, n % GROUP, some, :], in_=rotated[:])
+                out_group = out_rows[first * P : (first + GROUP) * P, :].rearrange("(p i) (b f) -> p (i b) f", i=GROUP, f=BANK)
+                pair_start = (n % GROUP - n % PAIR) * BANKS
+                nc.sync.dma_start(out=out_group[:, pair_start + first_bank : pair_start + first_bank + banks, :], in_=rotated[:])
 
             for h in range(HEADS):
                 nc.vector.scalar_tensor_tensor(
-                    out=bank_columns(products, h).rearrange("p a (j e) -> p a j e", e=2),
+                    out=products[
+                        :, (n % PAIR) * BANKS + h // HEADS_PER_BANK, :, (h % HEADS_PER_BANK) * HEAD_DIM : (h % HEADS_PER_BANK + 1) * HEAD_DIM
+                    ].rearrange("p a (j e) -> p a j e", e=2),
                     in0=head(n, h).rearrange("p (a j) -> p a j", a=2).unsqueeze(3).to_broadcast([P, 2, PAIRS, 2]),
                     scalar=inverse[:, h : h + 1],
                     in1=rot[:, n % TABLES, :].rearrange("p (a j e) -> p a j e", a=2, e=2),
                     op0=ALU.mult,
                     op1=ALU.mult,
                 )
-            if n < TILES - 1:
-                add_and_store(nc.gpsimd, 0, BANKS)
+            own_banks = (n % PAIR) * BANKS
+            if n < TILES - 2 * PAIR:
+                if n % PAIR == PAIR - 1:
+                    add_and_store(nc.gpsimd, 0, PAIR * BANKS)
+            elif n < TILES - 1:
+                add_and_store(nc.gpsimd, own_banks, BANKS)
             else:
                 for b in range(BANKS):
-                    add_and_store(nc.vector, b, 1)
+                    add_and_store(nc.vector, own_banks + b, 1)
 
         def when_valid(stage_of_tile, n):
             if 0 <= n < TILES:
                 stage_of_tile(n)
 
-        for step in range(-4, TILES):
-            when_valid(quantise_x, step + 2)
+        for step in range(-5, TILES):
+            if 0 <= step + 2 < PAIR:
+                quantise_x(step + 2, 1)
+            elif PAIR <= step + 2 < TILES and (step + 2) % PAIR == 0:
+                quantise_x(step + 2, PAIR)
             when_valid(multiply, step + 2)
-            when_valid(transpose_x, step + 4)
+            when_valid(transpose_x, step + 5)
             when_valid(sum_squares, step + 1)
             when_valid(inverse_rms_first_bank, step + 1)
-            when_valid(regroup_x, step + 3)
+            when_valid(regroup_x, step + 4)
             when_valid(inverse_rms_second_bank, step + 1)
             when_valid(rotate, step)

from contextlib import ExitStack

import concourse.mybir as mybir
from concourse.masks import make_identity

F32 = mybir.dt.float32
BF16 = mybir.dt.bfloat16
U32 = mybir.dt.uint32
U8 = mybir.dt.uint8
FP8X4 = mybir.dt.float8_e4m3fn_x4
ACT = mybir.ActivationFunctionType
ALU = mybir.AluOpType

P = 128
TOKENS = 4 * 1024
SEQUENCE = 1024
K = 1024
HEADS = 8
HEAD_DIM = 128
PAIRS = HEAD_DIM // 2
FEATURES = HEADS * HEAD_DIM
EPS = 1e-6

PACK = 4
PASSES = K // (P * PACK)
HALVES = 2
WORD_BLOCKS = PASSES * HALVES
BANK = 512
BANKS = FEATURES // BANK
HEADS_PER_BANK = BANK // HEAD_DIM
GROUP = 4
PAIR = 2
TILES = TOKENS // P
TABLES = SEQUENCE // P

FLOPS = 2 * TOKENS * K * FEATURES


def tile_mla_pb_t_kernel(tc, x, wq, q_norm_w, freqs_cos, freqs_sin, out):
    nc = tc.nc
    x_rows = x.flatten_outer_dims()
    out_rows = out.rearrange("b t h d -> (b t) (h d)")

    with ExitStack() as stack:
        keep = stack.enter_context(tc.tile_pool(name="keep", bufs=1))
        stage = stack.enter_context(tc.tile_pool(name="stage", bufs=2))
        work = stack.enter_context(tc.tile_pool(name="work", bufs=3))
        results = stack.enter_context(tc.tile_pool(name="results", bufs=6))
        psum_turned = stack.enter_context(tc.psum_pool(name="psum_turned", bufs=2))
        psum_q = stack.enter_context(tc.psum_pool(name="psum_q", bufs=3 * BANKS))
        stack.enter_context(tc.manual_schedule())

        gain_row = keep.tile([P, HEAD_DIM], BF16)
        nc.vector.memset(gain_row[:], 0.0)
        nc.sync.dma_start(out=gain_row[0:1, :], in_=q_norm_w.unsqueeze(0))
        cos = keep.tile([P, TABLES // GROUP, GROUP * PAIRS], BF16)
        sin = keep.tile([P, TABLES // GROUP, GROUP * PAIRS], BF16)
        for table, freqs in ((cos, freqs_cos), (sin, freqs_sin)):
            nc.scalar.dma_start(out=table[:], in_=freqs.rearrange("(s p i) j -> p s (i j)", p=P, i=GROUP))

        wq_sb = keep.tile([P, HEADS, K], BF16)
        wq_by_head = wq.rearrange("(h p) k -> p h k", p=P)
        for h in range(HEADS):
            nc.sync.dma_start(out=wq_sb[:, h, :], in_=wq_by_head[:, h, :])
        x_sb = keep.tile([P, TILES, K], BF16)
        for first in range(0, TILES, GROUP):
            x_group = x_rows[first * P : (first + GROUP) * P, :].rearrange("(p i) k -> p i k", i=GROUP)
            if first == 0:
                for i in range(GROUP):
                    nc.sync.dma_start(out=x_sb[:, i, :], in_=x_group[:, i, :])
            else:
                nc.sync.dma_start(out=x_sb[:, first : first + GROUP, :], in_=x_group)

        eps = keep.tile([P, 1], F32)
        nc.vector.memset(eps[:], EPS)
        first_use = keep.tile([P, 1], F32)
        nc.scalar.activation(out=first_use[:], in_=eps[:], func=ACT.Abs_reciprocal_sqrt)

        identity = keep.tile([P, P], F32)
        make_identity(nc, identity[:])
        evens_first = keep.tile([P, P], F32)
        nc.vector.tensor_copy(
            out=evens_first[:].rearrange("p (a j) -> p a j", a=2),
            in_=identity[:].rearrange("p (j a) -> p a j", a=2),
        )

        ones = keep.tile([P, P], BF16)
        nc.vector.memset(ones[:], 1.0)
        gain_bank = psum_turned.tile([P, WORD_BLOCKS, P], F32, tag="turned")
        nc.tensor.matmul(out=gain_bank[:, 0, :], lhsT=ones[:], rhs=gain_row[:], start=True, stop=True)
        gain = keep.tile([P, HEAD_DIM], F32)
        nc.vector.tensor_copy(out=gain[:], in_=gain_bank[:, 0, :])

        neg_sin = keep.tile([P, TABLES // GROUP, GROUP * PAIRS], BF16)
        nc.gpsimd.tensor_scalar(out=neg_sin[:], in0=sin[:], scalar1=-1.0, scalar2=0.0, op0=ALU.mult, op1=ALU.add)
        rot = keep.tile([P, TABLES, 2 * HEAD_DIM], F32)
        rot_parts = rot[:].rearrange("p m (a j e) -> p e a m j", a=2, e=2)
        gain_parts = gain[:].rearrange("p (j a) -> p a j", a=2)
        for e, a, trig in ((0, 0, cos), (0, 1, neg_sin), (1, 0, sin), (1, 1, cos)):
            nc.gpsimd.tensor_tensor(
                out=rot_parts[:, e, a],
                in0=trig[:].rearrange("p s (i j) -> p (s i) j", i=GROUP),
                in1=gain_parts[:, a].unsqueeze(1).to_broadcast([P, TABLES, PAIRS]),
                op=ALU.mult,
            )

        def turn(rows, selector):
            turned = psum_turned.tile([P, WORD_BLOCKS, P], F32)
            words = rows.bitcast(F32)
            for w in range(WORD_BLOCKS):
                nc.tensor.transpose(turned[:, w, :], words[:, w * P : (w + 1) * P], selector[:])
            return turned

        def by_packed_word(turned):
            return turned[:].rearrange("p (g u) r -> p g r u", u=HALVES)

        w_codes = keep.tile([P, PASSES, FEATURES], U32, align_bytes=64)
        w_scales = keep.tile([P, PASSES, FEATURES], U8, align_bytes=64)

        w_grouped_of = {}

        def regroup_w(h):
            turned = turn(wq_sb[:, h, :], evens_first)
            w_grouped = work.tile([P, PASSES * HEAD_DIM * PACK], BF16, align_bytes=64)
            words = w_grouped[:].bitcast(F32).rearrange("p (g r u) -> p g r u", g=PASSES, u=HALVES)
            if h % 2 == 0:
                nc.scalar.copy(out=words, in_=by_packed_word(turned))
            else:
                nc.vector.tensor_copy(out=words, in_=by_packed_word(turned))
            w_grouped_of[h] = w_grouped

        def quantise_w(h):
            features = slice(h * HEAD_DIM, (h + 1) * HEAD_DIM)
            for g in range(PASSES):
                nc.vector.quantize_mx(
                    out=w_codes[:, g, features].bitcast(FP8X4),
                    scales=w_scales[:, g, features],
                    in_=w_grouped_of[h][:, g * HEAD_DIM * PACK : (g + 1) * HEAD_DIM * PACK],
                )

        for h in range(HEADS + 1):
            if h < HEADS:
                regroup_w(h)
            if h > 0:
                quantise_w(h - 1)

        turned_of, q_of, squares_of, inverse_of = {}, {}, {}, {}
        grouped_of, codes_of, scales_of, products_of = {}, {}, {}, {}

        def transpose_x(n):
            turned_of[n] = turn(x_sb[:, n, :], identity)

        def regroup_x(n):
            if n % PAIR == 0:
                x_grouped = stage.tile([P, PAIR, PASSES * P * PACK], BF16, align_bytes=64)
                grouped_of[n // PAIR] = x_grouped
            nc.scalar.copy(
                out=grouped_of[n // PAIR][:, n % PAIR, :].bitcast(F32).rearrange("p (g r u) -> p g r u", g=PASSES, u=HALVES),
                in_=by_packed_word(turned_of[n]),
            )

        def quantise_x(n, count):
            if n % PAIR == 0:
                x_codes = stage.tile([P, PAIR, PASSES * P], U32, align_bytes=64)
                x_scales = stage.tile([P, PAIR, PASSES * P], U8, align_bytes=64)
                codes_of[n // PAIR], scales_of[n // PAIR] = x_codes, x_scales
            tiles = slice(n % PAIR, n % PAIR + count)
            nc.vector.quantize_mx(
                out=codes_of[n // PAIR][:, tiles, :].rearrange("p i c -> p (i c)").bitcast(FP8X4),
                scales=scales_of[n // PAIR][:, tiles, :].rearrange("p i c -> p (i c)"),
                in_=grouped_of[n // PAIR][:, tiles, :].rearrange("p i c -> p (i c)"),
            )

        def multiply(n):
            x_codes, x_scales = codes_of[n // PAIR][:, n % PAIR, :], scales_of[n // PAIR][:, n % PAIR, :]
            q_of[n] = []
            for b in range(BANKS):
                q_bank = psum_q.tile([P, BANK], F32)
                features = slice(b * BANK, (b + 1) * BANK)
                for g in range(PASSES):
                    tokens = slice(g * P, (g + 1) * P)
                    nc.tensor.matmul_mx(
                        out=q_bank[:],
                        lhsT=x_codes[:, tokens].bitcast(FP8X4),
                        lhsT_scale=x_scales[:, tokens],
                        rhs=w_codes[:, g, features].bitcast(FP8X4),
                        rhs_scale=w_scales[:, g, features],
                        start=(g == 0),
                        stop=(g == PASSES - 1),
                    )
                q_of[n].append(q_bank)

        def head(n, h):
            column = (h % HEADS_PER_BANK) * HEAD_DIM
            return q_of[n][h // HEADS_PER_BANK][:, column : column + HEAD_DIM]


        def sum_squares(n):
            squares = stage.tile([P, HEADS], F32)
            unread = stage.tile([P, FEATURES], BF16)
            for h in range(HEADS):
                nc.scalar.activation(
                    out=unread[:, h * HEAD_DIM : (h + 1) * HEAD_DIM],
                    in_=head(n, h),
                    func=ACT.Square,
                    accum_out=squares[:, h : h + 1],
                )
            squares_of[n] = squares

        def inverse_rms(n, b):
            if b == 0:
                inverse = stage.tile([P, HEADS], F32)
                inverse_of[n] = inverse
            heads = slice(b * HEADS_PER_BANK, (b + 1) * HEADS_PER_BANK)
            nc.scalar.activation(
                out=inverse_of[n][:, heads],
                in_=squares_of[n][:, heads],
                func=ACT.Abs_reciprocal_sqrt,
                scale=1.0 / HEAD_DIM,
                bias=eps[:],
            )

        def inverse_rms_first_bank(n):
            inverse_rms(n, 0)

        def inverse_rms_second_bank(n):
            inverse_rms(n, 1)

        def rotate(n):
            inverse = inverse_of[n]
            if n % PAIR == 0:
                new_products = work.tile([P, PAIR * BANKS, 2, BANK], F32)
                products_of[n // PAIR] = new_products
            products = products_of[n // PAIR]

            def add_and_store(adder, first_bank, banks):
                chosen = slice(first_bank, first_bank + banks)
                rotated = results.tile([P, banks, BANK], F32)
                adder.tensor_tensor(out=rotated[:], in0=products[:, chosen, 0, :], in1=products[:, chosen, 1, :], op=ALU.add)
                first = n - n % GROUP
                out_group = out_rows[first * P : (first + GROUP) * P, :].rearrange("(p i) (b f) -> p (i b) f", i=GROUP, f=BANK)
                pair_start = (n % GROUP - n % PAIR) * BANKS
                nc.sync.dma_start(out=out_group[:, pair_start + first_bank : pair_start + first_bank + banks, :], in_=rotated[:])

            for h in range(HEADS):
                nc.vector.scalar_tensor_tensor(
                    out=products[
                        :, (n % PAIR) * BANKS + h // HEADS_PER_BANK, :, (h % HEADS_PER_BANK) * HEAD_DIM : (h % HEADS_PER_BANK + 1) * HEAD_DIM
                    ].rearrange("p a (j e) -> p a j e", e=2),
                    in0=head(n, h).rearrange("p (a j) -> p a j", a=2).unsqueeze(3).to_broadcast([P, 2, PAIRS, 2]),
                    scalar=inverse[:, h : h + 1],
                    in1=rot[:, n % TABLES, :].rearrange("p (a j e) -> p a j e", a=2, e=2),
                    op0=ALU.mult,
                    op1=ALU.mult,
                )
            own_banks = (n % PAIR) * BANKS
            if n < TILES - 2 * PAIR:
                if n % PAIR == PAIR - 1:
                    add_and_store(nc.gpsimd, 0, PAIR * BANKS)
            elif n < TILES - 1:
                add_and_store(nc.gpsimd, own_banks, BANKS)
            else:
                for b in range(BANKS):
                    add_and_store(nc.vector, own_banks + b, 1)

        def when_valid(stage_of_tile, n):
            if 0 <= n < TILES:
                stage_of_tile(n)

        for step in range(-5, TILES):
            if 0 <= step + 2 < PAIR:
                quantise_x(step + 2, 1)
            elif PAIR <= step + 2 < TILES and (step + 2) % PAIR == 0:
                quantise_x(step + 2, PAIR)
            when_valid(multiply, step + 2)
            when_valid(transpose_x, step + 5)
            when_valid(sum_squares, step + 1)
            when_valid(inverse_rms_first_bank, step + 1)
            when_valid(regroup_x, step + 4)
            when_valid(inverse_rms_second_bank, step + 1)
            when_valid(rotate, step)
